import numpy as np
import ml_dtypes


def mxq(x, axis, fmt="e4m3"):
    dtype, down = {"e4m3": (ml_dtypes.float8_e4m3fn, 7), "e5m2": (ml_dtypes.float8_e5m2, 14)}[fmt]
    v = np.moveaxis(np.asarray(x, np.float32).astype(ml_dtypes.bfloat16).astype(np.float64), axis, -1)
    blocks = v.reshape(v.shape[:-1] + (-1, 32))
    amax = np.abs(blocks).max(-1, keepdims=True)
    byte = np.maximum(np.where(amax > 0, np.frexp(amax)[1] - 1 + 127, 0) - down, 1)
    scale = np.exp2(byte - 127.0)
    codes = (blocks / scale).astype(np.float32).astype(dtype).astype(np.float64)
    return np.moveaxis((codes * scale).reshape(v.shape), -1, axis)


WIDE = False


def mx_kscale(k):
    if not WIDE:
        return np.ones(k)
    levels = np.array([10, -10, 5, -5, 0])
    a = np.random.permutation(np.resize(levels, k // 512 * 4)).reshape(k // 512, 4)
    idx = np.arange(k)
    return np.exp2(a[idx // 512, idx % 128 // 32])


BF16 = ml_dtypes.bfloat16


def bf(x):
    return np.asarray(x, np.float32).astype(BF16)


def f64(x):
    return np.asarray(x).astype(np.float64)


B, G0, G1, C0, C1, NC = 8, 8, 4, 8192, 512, 58
NCH = 5 + 1 + NC
STRIDES = [8, 16]
SXY = [1.2, 1.1]
ANCH = [[[10, 13], [16, 30], [33, 23]], [[30, 61], [62, 45], [59, 119]]]
RAD = np.pi / 180.0
ANGLES = [RAD * a for a in (-60.0, -30.0, 0.0, 30.0, 60.0, 90.0)]
NA = len(ANCH[0]) * len(ANGLES)


def sigmoid(v):
    return 1.0 / (1.0 + np.exp(-v))


def _masked_anchors(level):
    s = STRIDES[level]
    return np.array([[w / s, h / s, a] for (w, h) in ANCH[level] for a in ANGLES], dtype=np.float64)


def _decode(feat, W, b, level):
    Bn, C, G, _ = feat.shape
    out = (mxq(W, 1, "e4m3") @ mxq(feat.reshape(Bn, C, G * G), 1, "e4m3")) + b[None, :, None]
    pred = out.reshape(Bn, NA, NCH, G, G).transpose(0, 1, 3, 4, 2)
    sxy = SXY[level]
    s = float(STRIDES[level])
    ma = _masked_anchors(level)
    aw = ma[:, 0][None, :, None, None]
    ah = ma[:, 1][None, :, None, None]
    aa = ma[:, 2][None, :, None, None]
    gx = np.arange(G, dtype=np.float64)[None, None, None, :]
    gy = np.arange(G, dtype=np.float64)[None, None, :, None]
    px = sigmoid(pred[..., 0]) * sxy - (sxy - 1.0) / 2.0 + gx
    py = sigmoid(pred[..., 1]) * sxy - (sxy - 1.0) / 2.0 + gy
    pw = np.exp(pred[..., 2]) * aw
    ph = np.exp(pred[..., 3]) * ah
    pa = pred[..., 4] + aa
    conf = sigmoid(pred[..., 5])
    cls = sigmoid(pred[..., 6:])
    boxes = np.stack([px * s, py * s, pw * s, ph * s, pa], axis=-1)
    out = np.concatenate([boxes, conf[..., None], cls], axis=-1)
    return out.reshape(Bn, -1, NCH)


def _draw_level(G, C):
    s = mx_kscale(C)
    g = np.full(NCH, 1.5)
    g[2:4] = 0.3
    x = np.random.standard_normal((B, C, G, G)) * s[None, :, None, None]
    W = np.random.standard_normal((NA, NCH, C)) * g[None, :, None] / np.sqrt(C) / s
    b = np.random.standard_normal((NA, NCH)) * 0.4
    b[:, 2:4] -= 2.0
    return bf(x), bf(W.reshape(NA * NCH, C)), bf(b.reshape(NA * NCH))


def setup_inputs():
    x0, W0, b0 = _draw_level(G0, C0)
    x1, W1, b1 = _draw_level(G1, C1)
    return {"x0": x0, "x1": x1, "W0": W0, "b0": b0, "W1": W1, "b1": b1}


def reference(x0, x1, W0, b0, W1, b1):
    o0 = _decode(f64(x0), f64(W0), f64(b0), 0)
    o1 = _decode(f64(x1), f64(W1), f64(b1), 1)
    return np.concatenate([o0, o1], axis=1)

@@ -1,0 +1,243 @@
+import math
+from contextlib import ExitStack
+
+import concourse.mybir as mybir
+from concourse.masks import make_identity
+
+F32 = mybir.dt.float32
+BF16 = mybir.dt.bfloat16
+I32 = mybir.dt.int32
+U32 = mybir.dt.uint32
+U8 = mybir.dt.uint8
+FP8X4 = mybir.dt.float8_e4m3fn_x4
+ALU = mybir.AluOpType
+ACT = mybir.ActivationFunctionType
+
+P = 128
+PACK = 4
+K_PASS = P * PACK
+PAIR = 2
+HALVES = PACK // PAIR
+BATCH = 8
+FIELDS = 64
+ANGLES = 6
+SHAPES = 3
+ANCHORS = SHAPES * ANGLES
+OUT_CH = ANCHORS * FIELDS
+BANK = 512
+CHUNKS = ((0, 512), (512, 512), (1024, 128))
+BANK_PASSES = BANK // (HALVES * P)
+SLAB = 4
+ANGLE_RAD = tuple(math.pi / 180.0 * a for a in (-60.0, -30.0, 0.0, 30.0, 60.0, 90.0))
+
+LEVELS = (
+    dict(grid=8, grid_bits=3, stride=8.0, sxy=1.2, shapes=((10, 13), (16, 30), (33, 23)), first_row=0),
+    dict(grid=4, grid_bits=2, stride=16.0, sxy=1.1, shapes=((30, 61), (62, 45), (59, 119)), first_row=ANCHORS * 64),
+)
+
+FLOPS = 2 * OUT_CH * (8192 * BATCH * 64 + 512 * BATCH * 16)
+
+
+def quantise_weights(nc, pools, ident, weights, codes, scales):
+    channels = weights.shape[1]
+    passes = channels // K_PASS
+    banks = 0
+    for o_tile in range(OUT_CH // P):
+        rows = slice(o_tile * P, (o_tile + 1) * P)
+        raw = pools["w_raw"].tile([P, channels], BF16, tag="w_raw")
+        nc.sync.dma_start(out=raw[:], in_=weights[rows, :])
+        words = raw[:].bitcast(F32)
+        for first in range(0, passes, BANK_PASSES):
+            n = min(BANK_PASSES, passes - first)
+            bank = pools["t_psum"].tile([P, BANK_PASSES, HALVES, P], F32, tag="bank")
+            for i in range(n):
+                for u in range(HALVES):
+                    col = ((first + i) * HALVES + u) * P
+                    nc.tensor.transpose(out=bank[:, i, u, :], in_=words[:, col : col + P], identity=ident[:])
+            grouped = pools["w_grouped"].tile([P, BANK_PASSES, P, PACK], BF16, tag="w_grouped", align_bytes=64)
+            dst = grouped[:, 0:n].bitcast(F32)
+            src = bank[:, 0:n].rearrange("p g u o -> p g o u")
+            if banks % 4 == 3:
+                nc.vector.tensor_copy(out=dst, in_=src)
+            else:
+                nc.scalar.copy(out=dst, in_=src)
+            banks += 1
+            for i in range(n):
+                nc.vector.quantize_mx(
+                    out=codes[:, first + i, rows].bitcast(FP8X4),
+                    scales=scales[:, first + i, rows],
+                    in_=grouped[:, i].rearrange("p o t -> p (o t)"),
+                )
+
+
+def quantise_features(nc, pools, feat, batches, first, n, codes, scales):
+    cells = feat.shape[2] * feat.shape[3]
+    grouped = pools["x_grouped"].tile([P, n, P, PACK], BF16, tag="x_grouped", align_bytes=64)
+    for i, b in enumerate(batches):
+        raw = pools["x_raw"].tile([P, n, PACK, cells], BF16, tag="x_raw")
+        nc.sync.dma_start(
+            out=raw[:].rearrange("p g (u e) w -> p (g u) (e w)", u=HALVES),
+            in_=feat[b, first * K_PASS : (first + n) * K_PASS].rearrange(
+                "(g u p e) h w -> p (g u) (e h w)", u=HALVES, p=P, e=PAIR
+            ),
+        )
+        dst = grouped[:, :, i * cells : (i + 1) * cells, :]
+        src = raw[:].rearrange("p g t w -> p g w t")
+        if i % 2 == 0:
+            nc.vector.tensor_copy(out=dst, in_=src)
+        else:
+            nc.scalar.copy(out=dst, in_=src)
+    nc.vector.quantize_mx(
+        out=codes[:, first : first + n, :].rearrange("p g c -> p (g c)").bitcast(FP8X4),
+        scales=scales[:, first : first + n, :].rearrange("p g c -> p (g c)"),
+        in_=grouped[:].rearrange("p g c t -> p (g c t)"),
+    )
+
+
+def level_constants(nc, pools, level, bias, ones, cell_index):
+    consts = pools["consts"]
+    tagged = "L%d" % level["grid"]
+    bias_row = consts.tile([P, OUT_CH], BF16, name="bias_row" + tagged)
+    nc.vector.memset(bias_row[:], 0.0)
+    nc.sync.dma_start(out=bias_row[0:1, :], in_=bias.rearrange("(r o) -> r o", r=1))
+    shift = consts.tile([P, OUT_CH], F32, name="shift" + tagged)
+    for start, width in CHUNKS:
+        spread = pools["acc_psum"].tile([P, BANK], F32, tag="acc", name="spread")
+        nc.tensor.matmul(
+            out=spread[:, :width], lhsT=ones[:], rhs=bias_row[:, start : start + width], start=True, stop=True
+        )
+        nc.vector.tensor_copy(out=shift[:, start : start + width], in_=spread[:, :width])
+    by_anchor = shift[:].rearrange("p (i j f) -> p i j f", i=SHAPES, j=ANGLES)
+    for j, angle in enumerate(ANGLE_RAD):
+        nc.vector.tensor_scalar_add(out=by_anchor[:, :, j, 4], in0=by_anchor[:, :, j, 4], scalar1=angle)
+    sizes = consts.tile([P, ANCHORS, 2], F32, name="sizes" + tagged)
+    for i, (w, h) in enumerate(level["shapes"]):
+        nc.vector.memset(sizes[:, i * ANGLES : (i + 1) * ANGLES, 0:1], float(w))
+        nc.vector.memset(sizes[:, i * ANGLES : (i + 1) * ANGLES, 1:2], float(h))
+    mask = level["grid"] - 1
+    cell = consts.tile([P, 2], I32, name="cell" + tagged)
+    nc.vector.tensor_single_scalar(out=cell[:, 0:1], in_=cell_index[:], scalar=mask, op=ALU.bitwise_and)
+    nc.vector.tensor_scalar(
+        out=cell[:, 1:2],
+        in0=cell_index[:],
+        scalar1=level["grid_bits"],
+        scalar2=mask,
+        op0=ALU.logical_shift_right,
+        op1=ALU.bitwise_and,
+    )
+    centre = consts.tile([P, 2], F32, name="centre" + tagged)
+    nc.vector.tensor_copy(out=centre[:], in_=cell[:])
+    nc.vector.tensor_scalar(
+        out=centre[:],
+        in0=centre[:],
+        scalar1=level["stride"],
+        scalar2=0.5 * level["stride"],
+        op0=ALU.mult,
+        op1=ALU.add,
+    )
+    return shift, sizes, centre
+
+
+def decode_and_store(nc, pools, level, constants, acc, start, width, batches, out):
+    shift, sizes, centre = constants
+    first_anchor = start // FIELDS
+    anchors = width // FIELDS
+    cells = level["grid"] * level["grid"]
+    work = pools["work"]
+    dec = work.tile([P, BANK // FIELDS, FIELDS], F32, tag="dec")
+    nc.vector.tensor_tensor(
+        out=dec[:, 0:anchors].rearrange("p a f -> p (a f)"),
+        in0=acc[:, :width],
+        in1=shift[:, start : start + width],
+        op=ALU.add,
+    )
+    th = work.tile([P, BANK // FIELDS, FIELDS], F32, tag="th")
+    nc.scalar.activation(out=th[:, 0:anchors], in_=dec[:, 0:anchors], func=ACT.Tanh, scale=0.5)
+    grown = work.tile([P, BANK // FIELDS, 2], F32, tag="grown")
+    nc.scalar.activation(out=grown[:, 0:anchors], in_=dec[:, 0:anchors, 2:4], func=ACT.Exp)
+    nc.vector.tensor_scalar(
+        out=dec[:, 0:anchors, 5:FIELDS],
+        in0=th[:, 0:anchors, 5:FIELDS],
+        scalar1=0.5,
+        scalar2=0.5,
+        op0=ALU.mult,
+        op1=ALU.add,
+    )
+    nc.vector.scalar_tensor_tensor(
+        out=dec[:, 0:anchors, 0:2],
+        in0=th[:, 0:anchors, 0:2],
+        scalar=0.5 * level["sxy"] * level["stride"],
+        in1=centre[:].unsqueeze(1).to_broadcast([P, anchors, 2]),
+        op0=ALU.mult,
+        op1=ALU.add,
+    )
+    nc.vector.tensor_tensor(
+        out=dec[:, 0:anchors, 2:4],
+        in0=grown[:, 0:anchors],
+        in1=sizes[:, first_anchor : first_anchor + anchors, :],
+        op=ALU.mult,
+    )
+    row = level["first_row"] + first_anchor * cells
+    for i, b in enumerate(batches):
+        nc.gpsimd.dma_start(
+            out=out[b, row : row + anchors * cells, :].rearrange("(a w) f -> w a f", a=anchors),
+            in_=dec[i * cells : (i + 1) * cells, 0:anchors, :],
+        )
+
+
+def detect(nc, pools, level, constants, feat, w_codes, w_scales, out):
+    passes = feat.shape[1] // K_PASS
+    per_tile = P // (level["grid"] * level["grid"])
+    for b0 in range(0, BATCH, per_tile):
+        batches = range(b0, b0 + per_tile)
+        x_codes = pools["x_codes"].tile([P, passes, P], U32, tag="x_codes", align_bytes=64)
+        x_scales = pools["x_codes"].tile([P, passes, P], U8, tag="x_scales", align_bytes=64)
+        accs = [pools["acc_psum"].tile([P, BANK], F32, tag="acc", name="acc%d" % c) for c in range(len(CHUNKS))]
+        for first in range(0, passes, SLAB):
+            n = min(SLAB, passes - first)
+            quantise_features(nc, pools, feat, batches, first, n, x_codes, x_scales)
+            for g in range(first, first + n):
+                for (start, width), acc in zip(CHUNKS, accs):
+                    nc.tensor.matmul_mx(
+                        out=acc[:, :width],
+                        lhsT=x_codes[:, g, :].bitcast(FP8X4),
+                        lhsT_scale=x_scales[:, g, :],
+                        rhs=w_codes[:, g, start : start + width].bitcast(FP8X4),
+                        rhs_scale=w_scales[:, g, start : start + width],
+                        start=(g == 0),
+                        stop=(g == passes - 1),
+                    )
+        for (start, width), acc in zip(CHUNKS, accs):
+            decode_and_store(nc, pools, level, constants, acc, start, width, batches, out)
+
+
+def tile_detect_k_kernel(tc, x0, x1, W0, b0, W1, b1, out):
+    nc = tc.nc
+    with ExitStack() as stack:
+        pools = dict(
+            consts=stack.enter_context(tc.tile_pool(name="consts", bufs=1)),
+            w_raw=stack.enter_context(tc.tile_pool(name="w_raw", bufs=3)),
+            w_grouped=stack.enter_context(tc.tile_pool(name="w_grouped", bufs=4)),
+            x_raw=stack.enter_context(tc.tile_pool(name="x_raw", bufs=8)),
+            x_grouped=stack.enter_context(tc.tile_pool(name="x_grouped", bufs=3)),
+            x_codes=stack.enter_context(tc.tile_pool(name="x_codes", bufs=2)),
+            work=stack.enter_context(tc.tile_pool(name="work", bufs=3)),
+            t_psum=stack.enter_context(tc.psum_pool(name="t_psum", bufs=4)),
+            acc_psum=stack.enter_context(tc.psum_pool(name="acc_psum", bufs=4)),
+        )
+        consts = pools["consts"]
+        ident = consts.tile([P, P], F32, name="ident")
+        make_identity(nc, ident[:])
+        ones = consts.tile([P, P], BF16, name="ones")
+        nc.vector.memset(ones[:], 1.0)
+        cell_index = consts.tile([P, 1], I32, name="cell_index")
+        nc.gpsimd.iota(cell_index[:], pattern=[[0, 1]], base=0, channel_multiplier=1)
+
+        for level, feat, weights, bias in ((LEVELS[1], x1, W1, b1), (LEVELS[0], x0, W0, b0)):
+            passes = weights.shape[1] // K_PASS
+            tagged = "L%d" % level["grid"]
+            w_codes = consts.tile([P, passes, OUT_CH], U32, name="w_codes" + tagged, align_bytes=64)
+            w_scales = consts.tile([P, passes, OUT_CH], U8, name="w_scales" + tagged, align_bytes=64)
+            quantise_weights(nc, pools, ident, weights, w_codes, w_scales)
+            constants = level_constants(nc, pools, level, bias, ones, cell_index)
+            detect(nc, pools, level, constants, feat, w_codes, w_scales, out)

@@ -24,10 +24,15 @@ ANGLES = 6
 SHAPES = 3
 ANCHORS = SHAPES * ANGLES
 OUT_CH = ANCHORS * FIELDS
+O_TILES = OUT_CH // P
 BANK = 512
+PSUM_BANKS = 8
 CHUNKS = ((0, 512), (512, 512), (1024, 128))
 BANK_PASSES = BANK // (HALVES * P)
 SLAB = 4
+LOAD_AHEAD = 6
+REGROUP_AHEAD = 3
+QUANTISE_AHEAD = 2
 ANGLE_RAD = tuple(math.pi / 180.0 * a for a in (-60.0, -30.0, 0.0, 30.0, 60.0, 90.0))
 
 LEVELS = (
@@ -38,71 +43,14 @@ LEVELS = (
 FLOPS = 2 * OUT_CH * (8192 * BATCH * 64 + 512 * BATCH * 16)
 
 
-def quantise_weights(nc, pools, ident, weights, codes, scales):
-    channels = weights.shape[1]
-    passes = channels // K_PASS
-    banks = 0
-    for o_tile in range(OUT_CH // P):
-        rows = slice(o_tile * P, (o_tile + 1) * P)
-        raw = pools["w_raw"].tile([P, channels], BF16, tag="w_raw")
-        nc.sync.dma_start(out=raw[:], in_=weights[rows, :])
-        words = raw[:].bitcast(F32)
-        for first in range(0, passes, BANK_PASSES):
-            n = min(BANK_PASSES, passes - first)
-            bank = pools["t_psum"].tile([P, BANK_PASSES, HALVES, P], F32, tag="bank")
-            for i in range(n):
-                for u in range(HALVES):
-                    col = ((first + i) * HALVES + u) * P
-                    nc.tensor.transpose(out=bank[:, i, u, :], in_=words[:, col : col + P], identity=ident[:])
-            grouped = pools["w_grouped"].tile([P, BANK_PASSES, P, PACK], BF16, tag="w_grouped", align_bytes=64)
-            dst = grouped[:, 0:n].bitcast(F32)
-            src = bank[:, 0:n].rearrange("p g u o -> p g o u")
-            if banks % 4 == 3:
-                nc.vector.tensor_copy(out=dst, in_=src)
-            else:
-                nc.scalar.copy(out=dst, in_=src)
-            banks += 1
-            for i in range(n):
-                nc.vector.quantize_mx(
-                    out=codes[:, first + i, rows].bitcast(FP8X4),
-                    scales=scales[:, first + i, rows],
-                    in_=grouped[:, i].rearrange("p o t -> p (o t)"),
-                )
-
-
-def quantise_features(nc, pools, feat, batches, first, n, codes, scales):
-    cells = feat.shape[2] * feat.shape[3]
-    grouped = pools["x_grouped"].tile([P, n, P, PACK], BF16, tag="x_grouped", align_bytes=64)
-    for i, b in enumerate(batches):
-        raw = pools["x_raw"].tile([P, n, PACK, cells], BF16, tag="x_raw")
-        nc.sync.dma_start(
-            out=raw[:].rearrange("p g (u e) w -> p (g u) (e w)", u=HALVES),
-            in_=feat[b, first * K_PASS : (first + n) * K_PASS].rearrange(
-                "(g u p e) h w -> p (g u) (e h w)", u=HALVES, p=P, e=PAIR
-            ),
-        )
-        dst = grouped[:, :, i * cells : (i + 1) * cells, :]
-        src = raw[:].rearrange("p g t w -> p g w t")
-        if i % 2 == 0:
-            nc.vector.tensor_copy(out=dst, in_=src)
-        else:
-            nc.scalar.copy(out=dst, in_=src)
-    nc.vector.quantize_mx(
-        out=codes[:, first : first + n, :].rearrange("p g c -> p (g c)").bitcast(FP8X4),
-        scales=scales[:, first : first + n, :].rearrange("p g c -> p (g c)"),
-        in_=grouped[:].rearrange("p g c t -> p (g c t)"),
-    )
-
-
-def level_constants(nc, pools, level, bias, ones, cell_index):
-    consts = pools["consts"]
+def level_constants(nc, consts, setup, psum, level, bias, ones, cell_index):
     tagged = "L%d" % level["grid"]
-    bias_row = consts.tile([P, OUT_CH], BF16, name="bias_row" + tagged)
+    bias_row = setup.tile([P, OUT_CH], BF16, name="bias_row" + tagged)
     nc.vector.memset(bias_row[:], 0.0)
     nc.sync.dma_start(out=bias_row[0:1, :], in_=bias.rearrange("(r o) -> r o", r=1))
     shift = consts.tile([P, OUT_CH], F32, name="shift" + tagged)
     for start, width in CHUNKS:
-        spread = pools["acc_psum"].tile([P, BANK], F32, tag="acc", name="spread")
+        spread = psum.tile([P, BANK], F32, tag="bank", name="spread")
         nc.tensor.matmul(
             out=spread[:, :width], lhsT=ones[:], rhs=bias_row[:, start : start + width], start=True, stop=True
         )
@@ -115,7 +63,7 @@ def level_constants(nc, pools, level, bias, ones, cell_index):
         nc.vector.memset(sizes[:, i * ANGLES : (i + 1) * ANGLES, 0:1], float(w))
         nc.vector.memset(sizes[:, i * ANGLES : (i + 1) * ANGLES, 1:2], float(h))
     mask = level["grid"] - 1
-    cell = consts.tile([P, 2], I32, name="cell" + tagged)
+    cell = setup.tile([P, 2], I32, name="cell" + tagged)
     nc.vector.tensor_single_scalar(out=cell[:, 0:1], in_=cell_index[:], scalar=mask, op=ALU.bitwise_and)
     nc.vector.tensor_scalar(
         out=cell[:, 1:2],
@@ -135,109 +83,239 @@ def level_constants(nc, pools, level, bias, ones, cell_index):
         op0=ALU.mult,
         op1=ALU.add,
     )
-    return shift, sizes, centre
+    return dict(shift=shift, sizes=sizes, centre=centre)
 
 
-def decode_and_store(nc, pools, level, constants, acc, start, width, batches, out):
-    shift, sizes, centre = constants
-    first_anchor = start // FIELDS
-    anchors = width // FIELDS
-    cells = level["grid"] * level["grid"]
-    work = pools["work"]
-    dec = work.tile([P, BANK // FIELDS, FIELDS], F32, tag="dec")
-    nc.vector.tensor_tensor(
-        out=dec[:, 0:anchors].rearrange("p a f -> p (a f)"),
-        in0=acc[:, :width],
-        in1=shift[:, start : start + width],
-        op=ALU.add,
-    )
-    th = work.tile([P, BANK // FIELDS, FIELDS], F32, tag="th")
-    nc.scalar.activation(out=th[:, 0:anchors], in_=dec[:, 0:anchors], func=ACT.Tanh, scale=0.5)
-    grown = work.tile([P, BANK // FIELDS, 2], F32, tag="grown")
-    nc.scalar.activation(out=grown[:, 0:anchors], in_=dec[:, 0:anchors, 2:4], func=ACT.Exp)
-    nc.vector.tensor_scalar(
-        out=dec[:, 0:anchors, 5:FIELDS],
-        in0=th[:, 0:anchors, 5:FIELDS],
-        scalar1=0.5,
-        scalar2=0.5,
-        op0=ALU.mult,
-        op1=ALU.add,
-    )
-    nc.vector.scalar_tensor_tensor(
-        out=dec[:, 0:anchors, 0:2],
-        in0=th[:, 0:anchors, 0:2],
-        scalar=0.5 * level["sxy"] * level["stride"],
-        in1=centre[:].unsqueeze(1).to_broadcast([P, anchors, 2]),
-        op0=ALU.mult,
-        op1=ALU.add,
-    )
-    nc.vector.tensor_tensor(
-        out=dec[:, 0:anchors, 2:4],
-        in0=grown[:, 0:anchors],
-        in1=sizes[:, first_anchor : first_anchor + anchors, :],
-        op=ALU.mult,
-    )
-    row = level["first_row"] + first_anchor * cells
-    for i, b in enumerate(batches):
-        nc.gpsimd.dma_start(
-            out=out[b, row : row + anchors * cells, :].rearrange("(a w) f -> w a f", a=anchors),
-            in_=dec[i * cells : (i + 1) * cells, 0:anchors, :],
+def quantise_bank(nc, copied, codes, scales):
+    for i in range(copied["n"]):
+        g = copied["first"] + i
+        nc.vector.quantize_mx(
+            out=codes[:, g, copied["cols"]].bitcast(FP8X4),
+            scales=scales[:, g, copied["cols"]],
+            in_=copied["grouped"][:, i].rearrange("p o t -> p (o t)"),
         )
 
 
-def detect(nc, pools, level, constants, feat, w_codes, w_scales, out):
-    passes = feat.shape[1] // K_PASS
-    per_tile = P // (level["grid"] * level["grid"])
-    for b0 in range(0, BATCH, per_tile):
-        batches = range(b0, b0 + per_tile)
-        x_codes = pools["x_codes"].tile([P, passes, P], U32, tag="x_codes", align_bytes=64)
-        x_scales = pools["x_codes"].tile([P, passes, P], U8, tag="x_scales", align_bytes=64)
-        accs = [pools["acc_psum"].tile([P, BANK], F32, tag="acc", name="acc%d" % c) for c in range(len(CHUNKS))]
-        for first in range(0, passes, SLAB):
-            n = min(SLAB, passes - first)
-            quantise_features(nc, pools, feat, batches, first, n, x_codes, x_scales)
-            for g in range(first, first + n):
-                for (start, width), acc in zip(CHUNKS, accs):
-                    nc.tensor.matmul_mx(
-                        out=acc[:, :width],
-                        lhsT=x_codes[:, g, :].bitcast(FP8X4),
-                        lhsT_scale=x_scales[:, g, :],
-                        rhs=w_codes[:, g, start : start + width].bitcast(FP8X4),
-                        rhs_scale=w_scales[:, g, start : start + width],
-                        start=(g == 0),
-                        stop=(g == passes - 1),
-                    )
-        for (start, width), acc in zip(CHUNKS, accs):
-            decode_and_store(nc, pools, level, constants, acc, start, width, batches, out)
+def quantise_weights(nc, pools, ident, weights, tiles_per_load, codes, scales):
+    channels = weights.shape[1]
+    passes = channels // K_PASS
+    banks = 0
+    copied = None
+    for first_tile in range(0, O_TILES, tiles_per_load):
+        raw = pools["w_raw"].tile([P, tiles_per_load, channels], BF16, tag="w_raw")
+        nc.sync.dma_start(
+            out=raw[:],
+            in_=weights[first_tile * P : (first_tile + tiles_per_load) * P, :].rearrange("(t p) c -> p t c", p=P),
+        )
+        for t in range(tiles_per_load):
+            words = raw[:, t, :].bitcast(F32)
+            for first in range(0, passes, BANK_PASSES):
+                n = min(BANK_PASSES, passes - first)
+                bank = pools["psum"].tile([P, BANK_PASSES, HALVES, P], F32, tag="bank", name="bank")
+                for i in range(n):
+                    for u in range(HALVES):
+                        lo = (first + i) * HALVES * P
+                        nc.tensor.transpose(
+                            out=bank[:, i, u, :], in_=words[:, lo + u : lo + HALVES * P : HALVES], identity=ident[:]
+                        )
+                grouped = pools["w_grouped"].tile([P, BANK_PASSES, P, PACK], BF16, tag="w_grouped", align_bytes=64)
+                dst = grouped[:, 0:n].bitcast(F32)
+                src = bank[:, 0:n].rearrange("p g u o -> p g o u")
+                if banks % 4 == 3:
+                    nc.vector.tensor_copy(out=dst, in_=src)
+                else:
+                    nc.scalar.copy(out=dst, in_=src)
+                banks += 1
+                if copied is not None:
+                    quantise_bank(nc, copied, codes, scales)
+                o_tile = first_tile + t
+                copied = dict(grouped=grouped, first=first, n=n, cols=slice(o_tile * P, (o_tile + 1) * P))
+    quantise_bank(nc, copied, codes, scales)
+
+
+def load_features(nc, pools, slab):
+    job = slab["job"]
+    feat = job["feat"]
+    cells = job["cells"]
+    channels = slice(slab["first"] * K_PASS, (slab["first"] + slab["n"]) * K_PASS)
+    for b in job["batches"]:
+        raw = pools["x_raw"].tile([P, slab["n"], PACK, cells], BF16, tag="x_raw%d" % cells, name="x_raw")
+        nc.sync.dma_start(
+            out=raw[:].rearrange("p g t w -> p g (t w)"),
+            in_=feat[b, channels].rearrange("(g p t) h w -> p g (t h w)", p=P, t=PACK),
+        )
+        slab["raw"].append(raw)
+
+
+def regroup_features(nc, pools, slab):
+    cells = slab["job"]["cells"]
+    grouped = pools["x_grouped"].tile([P, slab["n"], P, PACK], BF16, tag="x_grouped", align_bytes=64)
+    for i, raw in enumerate(slab["raw"]):
+        dst = grouped[:, :, i * cells : (i + 1) * cells, :]
+        src = raw[:].rearrange("p g t w -> p g w t")
+        if i % 2 == 0:
+            nc.vector.tensor_copy(out=dst, in_=src)
+        else:
+            nc.scalar.copy(out=dst, in_=src)
+    slab["grouped"] = grouped
+
+
+def quantise_features(nc, pools, slab):
+    job = slab["job"]
+    if slab["first"] == 0:
+        job["codes"] = pools["x_codes"].tile([P, job["passes"], P], U32, tag="x_codes", name="x_codes", align_bytes=64)
+        job["scales"] = pools["x_codes"].tile([P, job["passes"], P], U8, tag="x_scales", name="x_scales", align_bytes=64)
+    passes = slice(slab["first"], slab["first"] + slab["n"])
+    nc.vector.quantize_mx(
+        out=job["codes"][:, passes, :].rearrange("p g c -> p (g c)").bitcast(FP8X4),
+        scales=job["scales"][:, passes, :].rearrange("p g c -> p (g c)"),
+        in_=slab["grouped"][:].rearrange("p g c t -> p (g c t)"),
+    )
+
+
+def multiply(nc, pools, slab):
+    job = slab["job"]
+    if slab["first"] == 0:
+        job["accs"] = [pools["psum"].tile([P, BANK], F32, tag="bank", name="acc%d" % c) for c in range(len(CHUNKS))]
+    for (start, width), acc in zip(CHUNKS, job["accs"]):
+        for g in range(slab["first"], slab["first"] + slab["n"]):
+            nc.tensor.matmul_mx(
+                out=acc[:, :width],
+                lhsT=job["codes"][:, g, :].bitcast(FP8X4),
+                lhsT_scale=job["scales"][:, g, :],
+                rhs=job["w_codes"][:, g, start : start + width].bitcast(FP8X4),
+                rhs_scale=job["w_scales"][:, g, start : start + width],
+                start=(g == 0),
+                stop=(g == job["passes"] - 1),
+            )
+
+
+def decode_first(nc, pools, job):
+    work = pools["work"]
+    for (start, width), acc in zip(CHUNKS, job["accs"]):
+        anchors = width // FIELDS
+        dec = work.tile([P, BANK // FIELDS, FIELDS], F32, tag="dec", name="dec", bufs=2 * len(CHUNKS))
+        nc.vector.tensor_tensor(
+            out=dec[:, 0:anchors].rearrange("p a f -> p (a f)"),
+            in0=acc[:, :width],
+            in1=job["constants"]["shift"][:, start : start + width],
+            op=ALU.add,
+        )
+        th = work.tile([P, BANK // FIELDS, FIELDS], F32, tag="th", name="th", bufs=len(CHUNKS))
+        nc.scalar.activation(out=th[:, 0:anchors], in_=dec[:, 0:anchors], func=ACT.Tanh, scale=0.5)
+        grown = work.tile([P, BANK // FIELDS, 2], F32, tag="grown", name="grown", bufs=len(CHUNKS))
+        nc.scalar.activation(out=grown[:, 0:anchors], in_=dec[:, 0:anchors, 2:4], func=ACT.Exp)
+        job["decoding"].append((dec, th, grown))
+
+
+def decode_second(nc, job, out):
+    level = job["level"]
+    cells = job["cells"]
+    for (start, width), (dec, th, grown) in zip(CHUNKS, job["decoding"]):
+        first_anchor = start // FIELDS
+        anchors = width // FIELDS
+        nc.vector.tensor_scalar(
+            out=dec[:, 0:anchors, 5:FIELDS],
+            in0=th[:, 0:anchors, 5:FIELDS],
+            scalar1=0.5,
+            scalar2=0.5,
+            op0=ALU.mult,
+            op1=ALU.add,
+        )
+        nc.vector.scalar_tensor_tensor(
+            out=dec[:, 0:anchors, 0:2],
+            in0=th[:, 0:anchors, 0:2],
+            scalar=0.5 * level["sxy"] * level["stride"],
+            in1=job["constants"]["centre"][:].unsqueeze(1).to_broadcast([P, anchors, 2]),
+            op0=ALU.mult,
+            op1=ALU.add,
+        )
+        nc.vector.tensor_tensor(
+            out=dec[:, 0:anchors, 2:4],
+            in0=grown[:, 0:anchors],
+            in1=job["constants"]["sizes"][:, first_anchor : first_anchor + anchors, :],
+            op=ALU.mult,
+        )
+        row = level["first_row"] + first_anchor * cells
+        for i, b in enumerate(job["batches"]):
+            nc.sync.dma_start(
+                out=out[b, row : row + anchors * cells, :].rearrange("(a w) f -> w a f", a=anchors),
+                in_=dec[i * cells : (i + 1) * cells, 0:anchors, :],
+            )
 
 
 def tile_detect_k_kernel(tc, x0, x1, W0, b0, W1, b1, out):
     nc = tc.nc
+    feats = (x0, x1)
+    weights = (W0, W1)
+    biases = (b0, b1)
     with ExitStack() as stack:
-        pools = dict(
-            consts=stack.enter_context(tc.tile_pool(name="consts", bufs=1)),
-            w_raw=stack.enter_context(tc.tile_pool(name="w_raw", bufs=3)),
-            w_grouped=stack.enter_context(tc.tile_pool(name="w_grouped", bufs=4)),
-            x_raw=stack.enter_context(tc.tile_pool(name="x_raw", bufs=8)),
-            x_grouped=stack.enter_context(tc.tile_pool(name="x_grouped", bufs=3)),
-            x_codes=stack.enter_context(tc.tile_pool(name="x_codes", bufs=2)),
-            work=stack.enter_context(tc.tile_pool(name="work", bufs=3)),
-            t_psum=stack.enter_context(tc.psum_pool(name="t_psum", bufs=4)),
-            acc_psum=stack.enter_context(tc.psum_pool(name="acc_psum", bufs=4)),
-        )
-        consts = pools["consts"]
+        stack.enter_context(tc.manual_schedule())
+        consts = stack.enter_context(tc.tile_pool(name="consts", bufs=1))
+        psum = stack.enter_context(tc.psum_pool(name="psum", bufs=PSUM_BANKS))
+
         ident = consts.tile([P, P], F32, name="ident")
         make_identity(nc, ident[:])
         ones = consts.tile([P, P], BF16, name="ones")
         nc.vector.memset(ones[:], 1.0)
         cell_index = consts.tile([P, 1], I32, name="cell_index")
         nc.gpsimd.iota(cell_index[:], pattern=[[0, 1]], base=0, channel_multiplier=1)
+        with tc.tile_pool(name="setup", bufs=1) as setup:
+            constants = [
+                level_constants(nc, consts, setup, psum, LEVELS[lv], biases[lv], ones, cell_index) for lv in (0, 1)
+            ]
 
-        for level, feat, weights, bias in ((LEVELS[1], x1, W1, b1), (LEVELS[0], x0, W0, b0)):
-            passes = weights.shape[1] // K_PASS
-            tagged = "L%d" % level["grid"]
-            w_codes = consts.tile([P, passes, OUT_CH], U32, name="w_codes" + tagged, align_bytes=64)
-            w_scales = consts.tile([P, passes, OUT_CH], U8, name="w_scales" + tagged, align_bytes=64)
-            quantise_weights(nc, pools, ident, weights, w_codes, w_scales)
-            constants = level_constants(nc, pools, level, bias, ones, cell_index)
-            detect(nc, pools, level, constants, feat, w_codes, w_scales, out)
+        pools = dict(
+            psum=psum,
+            w_raw=stack.enter_context(tc.tile_pool(name="w_raw", bufs=3)),
+            w_grouped=stack.enter_context(tc.tile_pool(name="w_grouped", bufs=4)),
+            x_raw=stack.enter_context(tc.tile_pool(name="x_raw", bufs=8)),
+            x_grouped=stack.enter_context(tc.tile_pool(name="x_grouped", bufs=3)),
+            x_codes=stack.enter_context(tc.tile_pool(name="x_codes", bufs=2)),
+            work=stack.enter_context(tc.tile_pool(name="work", bufs=3)),
+        )
+
+        w_codes = [None, None]
+        w_scales = [None, None]
+        for lv, tiles_per_load in ((1, O_TILES), (0, 1)):
+            passes = weights[lv].shape[1] // K_PASS
+            w_codes[lv] = consts.tile([P, passes, OUT_CH], U32, name="w_codes%d" % lv, align_bytes=64)
+            w_scales[lv] = consts.tile([P, passes, OUT_CH], U8, name="w_scales%d" % lv, align_bytes=64)
+            quantise_weights(nc, pools, ident, weights[lv], tiles_per_load, w_codes[lv], w_scales[lv])
+
+        slabs = []
+        for lv in (1, 0):
+            cells = LEVELS[lv]["grid"] * LEVELS[lv]["grid"]
+            passes = feats[lv].shape[1] // K_PASS
+            for b in range(0, BATCH, P // cells):
+                job = dict(
+                    level=LEVELS[lv],
+                    constants=constants[lv],
+                    feat=feats[lv],
+                    cells=cells,
+                    passes=passes,
+                    batches=range(b, b + P // cells),
+                    w_codes=w_codes[lv],
+                    w_scales=w_scales[lv],
+                    decoding=[],
+                )
+                for first in range(0, passes, SLAB):
+                    n = min(SLAB, passes - first)
+                    slabs.append(dict(job=job, first=first, n=n, last=(first + n == passes), raw=[]))
+
+        def slab_at(k):
+            return slabs[k] if 0 <= k < len(slabs) else None
+
+        for step in range(-LOAD_AHEAD, len(slabs) + 2):
+            if slab_at(step + LOAD_AHEAD) is not None:
+                load_features(nc, pools, slab_at(step + LOAD_AHEAD))
+            if slab_at(step + QUANTISE_AHEAD) is not None:
+                quantise_features(nc, pools, slab_at(step + QUANTISE_AHEAD))
+            if slab_at(step + REGROUP_AHEAD) is not None:
+                regroup_features(nc, pools, slab_at(step + REGROUP_AHEAD))
+            if slab_at(step - 2) is not None and slab_at(step - 2)["last"]:
+                decode_second(nc, slab_at(step - 2)["job"], out)
+            if slab_at(step) is not None:
+                multiply(nc, pools, slab_at(step))
+            if slab_at(step - 1) is not None and slab_at(step - 1)["last"]:
+                decode_first(nc, pools, slab_at(step - 1)["job"])

@@ -29,6 +29,7 @@ BANK = 512
 PSUM_BANKS = 8
 CHUNKS = ((0, 512), (512, 512), (1024, 128))
 BANK_PASSES = BANK // (HALVES * P)
+LOAD_CHANNELS = 4096
 SLAB = 4
 LOAD_AHEAD = 6
 REGROUP_AHEAD = 3
@@ -43,27 +44,14 @@ LEVELS = (
 FLOPS = 2 * OUT_CH * (8192 * BATCH * 64 + 512 * BATCH * 16)
 
 
-def level_constants(nc, consts, setup, psum, level, bias, ones, cell_index):
+def anchor_constants(nc, consts, level, cell_index):
     tagged = "L%d" % level["grid"]
-    bias_row = setup.tile([P, OUT_CH], BF16, name="bias_row" + tagged)
-    nc.vector.memset(bias_row[:], 0.0)
-    nc.sync.dma_start(out=bias_row[0:1, :], in_=bias.rearrange("(r o) -> r o", r=1))
-    shift = consts.tile([P, OUT_CH], F32, name="shift" + tagged)
-    for start, width in CHUNKS:
-        spread = psum.tile([P, BANK], F32, tag="bank", name="spread")
-        nc.tensor.matmul(
-            out=spread[:, :width], lhsT=ones[:], rhs=bias_row[:, start : start + width], start=True, stop=True
-        )
-        nc.vector.tensor_copy(out=shift[:, start : start + width], in_=spread[:, :width])
-    by_anchor = shift[:].rearrange("p (i j f) -> p i j f", i=SHAPES, j=ANGLES)
-    for j, angle in enumerate(ANGLE_RAD):
-        nc.vector.tensor_scalar_add(out=by_anchor[:, :, j, 4], in0=by_anchor[:, :, j, 4], scalar1=angle)
     sizes = consts.tile([P, ANCHORS, 2], F32, name="sizes" + tagged)
     for i, (w, h) in enumerate(level["shapes"]):
         nc.vector.memset(sizes[:, i * ANGLES : (i + 1) * ANGLES, 0:1], float(w))
         nc.vector.memset(sizes[:, i * ANGLES : (i + 1) * ANGLES, 1:2], float(h))
     mask = level["grid"] - 1
-    cell = setup.tile([P, 2], I32, name="cell" + tagged)
+    cell = consts.tile([P, 2], I32, name="cell" + tagged)
     nc.vector.tensor_single_scalar(out=cell[:, 0:1], in_=cell_index[:], scalar=mask, op=ALU.bitwise_and)
     nc.vector.tensor_scalar(
         out=cell[:, 1:2],
@@ -83,7 +71,28 @@ def level_constants(nc, consts, setup, psum, level, bias, ones, cell_index):
         op0=ALU.mult,
         op1=ALU.add,
     )
-    return dict(shift=shift, sizes=sizes, centre=centre)
+    return sizes, centre
+
+
+def load_bias_row(nc, consts, level, bias):
+    bias_row = consts.tile([P, OUT_CH], BF16, name="bias_rowL%d" % level["grid"])
+    nc.vector.memset(bias_row[:], 0.0)
+    nc.sync.dma_start(out=bias_row[0:1, :], in_=bias.rearrange("(r o) -> r o", r=1))
+    return bias_row
+
+
+def spread_bias(nc, consts, psum, level, bias_row, ones):
+    shift = consts.tile([P, OUT_CH], F32, name="shiftL%d" % level["grid"])
+    for start, width in CHUNKS:
+        spread = psum.tile([P, BANK], F32, tag="bank", name="spread")
+        nc.tensor.matmul(
+            out=spread[:, :width], lhsT=ones[:], rhs=bias_row[:, start : start + width], start=True, stop=True
+        )
+        nc.vector.tensor_copy(out=shift[:, start : start + width], in_=spread[:, :width])
+    by_anchor = shift[:].rearrange("p (i j f) -> p i j f", i=SHAPES, j=ANGLES)
+    for j, angle in enumerate(ANGLE_RAD):
+        nc.vector.tensor_scalar_add(out=by_anchor[:, :, j, 4], in0=by_anchor[:, :, j, 4], scalar1=angle)
+    return shift
 
 
 def quantise_bank(nc, copied, codes, scales):
@@ -96,21 +105,21 @@ def quantise_bank(nc, copied, codes, scales):
         )
 
 
-def quantise_weights(nc, pools, ident, weights, tiles_per_load, codes, scales):
+def quantise_weights(nc, pools, ident, weights, codes, scales):
     channels = weights.shape[1]
-    passes = channels // K_PASS
+    load_passes = min(channels, LOAD_CHANNELS) // K_PASS
     banks = 0
     copied = None
-    for first_tile in range(0, O_TILES, tiles_per_load):
-        raw = pools["w_raw"].tile([P, tiles_per_load, channels], BF16, tag="w_raw")
-        nc.sync.dma_start(
-            out=raw[:],
-            in_=weights[first_tile * P : (first_tile + tiles_per_load) * P, :].rearrange("(t p) c -> p t c", p=P),
-        )
-        for t in range(tiles_per_load):
-            words = raw[:, t, :].bitcast(F32)
-            for first in range(0, passes, BANK_PASSES):
-                n = min(BANK_PASSES, passes - first)
+    for o_tile in range(O_TILES):
+        rows = slice(o_tile * P, (o_tile + 1) * P)
+        for load_first in range(0, channels // K_PASS, load_passes):
+            raw = pools["w_raw"].tile([P, load_passes * K_PASS], BF16, tag="w_raw")
+            nc.sync.dma_start(
+                out=raw[:], in_=weights[rows, load_first * K_PASS : (load_first + load_passes) * K_PASS]
+            )
+            words = raw[:].bitcast(F32)
+            for first in range(0, load_passes, BANK_PASSES):
+                n = min(BANK_PASSES, load_passes - first)
                 bank = pools["psum"].tile([P, BANK_PASSES, HALVES, P], F32, tag="bank", name="bank")
                 for i in range(n):
                     for u in range(HALVES):
@@ -128,8 +137,7 @@ def quantise_weights(nc, pools, ident, weights, tiles_per_load, codes, scales):
                 banks += 1
                 if copied is not None:
                     quantise_bank(nc, copied, codes, scales)
-                o_tile = first_tile + t
-                copied = dict(grouped=grouped, first=first, n=n, cols=slice(o_tile * P, (o_tile + 1) * P))
+                copied = dict(grouped=grouped, first=load_first + first, n=n, cols=rows)
     quantise_bank(nc, copied, codes, scales)
 
 
@@ -260,14 +268,14 @@ def tile_detect_k_kernel(tc, x0, x1, W0, b0, W1, b1, out):
         nc.vector.memset(ones[:], 1.0)
         cell_index = consts.tile([P, 1], I32, name="cell_index")
         nc.gpsimd.iota(cell_index[:], pattern=[[0, 1]], base=0, channel_multiplier=1)
-        with tc.tile_pool(name="setup", bufs=1) as setup:
-            constants = [
-                level_constants(nc, consts, setup, psum, LEVELS[lv], biases[lv], ones, cell_index) for lv in (0, 1)
-            ]
+        bias_rows = [load_bias_row(nc, consts, LEVELS[lv], biases[lv]) for lv in (0, 1)]
+        anchor_tiles = [anchor_constants(nc, consts, LEVELS[lv], cell_index) for lv in (0, 1)]
+        shifts = [spread_bias(nc, consts, psum, LEVELS[lv], bias_rows[lv], ones) for lv in (0, 1)]
+        constants = [dict(shift=shifts[lv], sizes=anchor_tiles[lv][0], centre=anchor_tiles[lv][1]) for lv in (0, 1)]
 
         pools = dict(
             psum=psum,
-            w_raw=stack.enter_context(tc.tile_pool(name="w_raw", bufs=3)),
+            w_raw=stack.enter_context(tc.tile_pool(name="w_raw", bufs=6)),
             w_grouped=stack.enter_context(tc.tile_pool(name="w_grouped", bufs=4)),
             x_raw=stack.enter_context(tc.tile_pool(name="x_raw", bufs=8)),
             x_grouped=stack.enter_context(tc.tile_pool(name="x_grouped", bufs=3)),
@@ -277,11 +285,11 @@ def tile_detect_k_kernel(tc, x0, x1, W0, b0, W1, b1, out):
 
         w_codes = [None, None]
         w_scales = [None, None]
-        for lv, tiles_per_load in ((1, O_TILES), (0, 1)):
+        for lv in (1, 0):
             passes = weights[lv].shape[1] // K_PASS
             w_codes[lv] = consts.tile([P, passes, OUT_CH], U32, name="w_codes%d" % lv, align_bytes=64)
             w_scales[lv] = consts.tile([P, passes, OUT_CH], U8, name="w_scales%d" % lv, align_bytes=64)
-            quantise_weights(nc, pools, ident, weights[lv], tiles_per_load, w_codes[lv], w_scales[lv])
+            quantise_weights(nc, pools, ident, weights[lv], w_codes[lv], w_scales[lv])
 
         slabs = []
         for lv in (1, 0):

@@ -76,7 +76,7 @@ def anchor_constants(nc, consts, level, cell_index):
 
 def load_bias_row(nc, consts, level, bias):
     bias_row = consts.tile([P, OUT_CH], BF16, name="bias_rowL%d" % level["grid"])
-    nc.vector.memset(bias_row[:], 0.0)
+    nc.vector.memset(bias_row[:].bitcast(I32), 0)
     nc.sync.dma_start(out=bias_row[0:1, :], in_=bias.rearrange("(r o) -> r o", r=1))
     return bias_row
 
@@ -108,36 +108,44 @@ def quantise_bank(nc, copied, codes, scales):
 def quantise_weights(nc, pools, ident, weights, codes, scales):
     channels = weights.shape[1]
     load_passes = min(channels, LOAD_CHANNELS) // K_PASS
+    tiles_per_load = LOAD_CHANNELS // (load_passes * K_PASS)
     banks = 0
     copied = None
-    for o_tile in range(O_TILES):
-        rows = slice(o_tile * P, (o_tile + 1) * P)
+    for first_tile in range(0, O_TILES, tiles_per_load):
+        tiles = min(tiles_per_load, O_TILES - first_tile)
         for load_first in range(0, channels // K_PASS, load_passes):
-            raw = pools["w_raw"].tile([P, load_passes * K_PASS], BF16, tag="w_raw")
+            raw = pools["w_raw"].tile([P, tiles, load_passes * K_PASS], BF16, tag="w_raw")
             nc.sync.dma_start(
-                out=raw[:], in_=weights[rows, load_first * K_PASS : (load_first + load_passes) * K_PASS]
+                out=raw[:],
+                in_=weights[
+                    first_tile * P : (first_tile + tiles) * P, load_first * K_PASS : (load_first + load_passes) * K_PASS
+                ].rearrange("(t p) c -> p t c", p=P),
             )
-            words = raw[:].bitcast(F32)
-            for first in range(0, load_passes, BANK_PASSES):
-                n = min(BANK_PASSES, load_passes - first)
-                bank = pools["psum"].tile([P, BANK_PASSES, HALVES, P], F32, tag="bank", name="bank")
-                for i in range(n):
-                    for u in range(HALVES):
-                        lo = (first + i) * HALVES * P
-                        nc.tensor.transpose(
-                            out=bank[:, i, u, :], in_=words[:, lo + u : lo + HALVES * P : HALVES], identity=ident[:]
-                        )
-                grouped = pools["w_grouped"].tile([P, BANK_PASSES, P, PACK], BF16, tag="w_grouped", align_bytes=64)
-                dst = grouped[:, 0:n].bitcast(F32)
-                src = bank[:, 0:n].rearrange("p g u o -> p g o u")
-                if banks % 4 == 3:
-                    nc.vector.tensor_copy(out=dst, in_=src)
-                else:
-                    nc.scalar.copy(out=dst, in_=src)
-                banks += 1
-                if copied is not None:
-                    quantise_bank(nc, copied, codes, scales)
-                copied = dict(grouped=grouped, first=load_first + first, n=n, cols=rows)
+            for t in range(tiles):
+                words = raw[:, t, :].bitcast(F32)
+                for first in range(0, load_passes, BANK_PASSES):
+                    n = min(BANK_PASSES, load_passes - first)
+                    bank = pools["psum"].tile([P, BANK_PASSES, HALVES, P], F32, tag="bank", name="bank")
+                    for i in range(n):
+                        for u in range(HALVES):
+                            lo = (first + i) * HALVES * P
+                            nc.tensor.transpose(
+                                out=bank[:, i, u, :], in_=words[:, lo + u : lo + HALVES * P : HALVES], identity=ident[:]
+                            )
+                    grouped = pools["w_grouped"].tile([P, BANK_PASSES, P, PACK], BF16, tag="w_grouped", align_bytes=64)
+                    dst = grouped[:, 0:n].bitcast(F32)
+                    src = bank[:, 0:n].rearrange("p g u o -> p g o u")
+                    if banks % 4 == 3:
+                        nc.vector.tensor_copy(out=dst, in_=src)
+                    else:
+                        nc.scalar.copy(out=dst, in_=src)
+                    banks += 1
+                    if copied is not None:
+                        quantise_bank(nc, copied, codes, scales)
+                    o_tile = first_tile + t
+                    copied = dict(
+                        grouped=grouped, first=load_first + first, n=n, cols=slice(o_tile * P, (o_tile + 1) * P)
+                    )
     quantise_bank(nc, copied, codes, scales)
 
 
@@ -262,13 +270,13 @@ def tile_detect_k_kernel(tc, x0, x1, W0, b0, W1, b1, out):
         consts = stack.enter_context(tc.tile_pool(name="consts", bufs=1))
         psum = stack.enter_context(tc.psum_pool(name="psum", bufs=PSUM_BANKS))
 
+        bias_rows = [load_bias_row(nc, consts, LEVELS[lv], biases[lv]) for lv in (0, 1)]
         ident = consts.tile([P, P], F32, name="ident")
         make_identity(nc, ident[:])
         ones = consts.tile([P, P], BF16, name="ones")
         nc.vector.memset(ones[:], 1.0)
         cell_index = consts.tile([P, 1], I32, name="cell_index")
         nc.gpsimd.iota(cell_index[:], pattern=[[0, 1]], base=0, channel_multiplier=1)
-        bias_rows = [load_bias_row(nc, consts, LEVELS[lv], biases[lv]) for lv in (0, 1)]
         anchor_tiles = [anchor_constants(nc, consts, LEVELS[lv], cell_index) for lv in (0, 1)]
         shifts = [spread_bias(nc, consts, psum, LEVELS[lv], bias_rows[lv], ones) for lv in (0, 1)]
         constants = [dict(shift=shifts[lv], sizes=anchor_tiles[lv][0], centre=anchor_tiles[lv][1]) for lv in (0, 1)]

@@ -28,8 +28,9 @@ O_TILES = OUT_CH // P
 BANK = 512
 PSUM_BANKS = 8
 CHUNKS = ((0, 512), (512, 512), (1024, 128))
-BANK_PASSES = BANK // (HALVES * P)
-LOAD_CHANNELS = 4096
+BANK_TILES = BANK // (HALVES * P)
+LOAD_VALUES = 8192
+VECTOR_EVERY = 6
 SLAB = 4
 LOAD_AHEAD = 6
 REGROUP_AHEAD = 3
@@ -96,56 +97,50 @@ def spread_bias(nc, consts, psum, level, bias_row, ones):
 
 
 def quantise_bank(nc, copied, codes, scales):
-    for i in range(copied["n"]):
-        g = copied["first"] + i
-        nc.vector.quantize_mx(
-            out=codes[:, g, copied["cols"]].bitcast(FP8X4),
-            scales=scales[:, g, copied["cols"]],
-            in_=copied["grouped"][:, i].rearrange("p o t -> p (o t)"),
-        )
+    nc.vector.quantize_mx(
+        out=codes[:, copied["g"], copied["cols"]].bitcast(FP8X4),
+        scales=scales[:, copied["g"], copied["cols"]],
+        in_=copied["grouped"].rearrange("p k o t -> p (k o t)"),
+    )
 
 
 def quantise_weights(nc, pools, ident, weights, codes, scales):
     channels = weights.shape[1]
-    load_passes = min(channels, LOAD_CHANNELS) // K_PASS
-    tiles_per_load = LOAD_CHANNELS // (load_passes * K_PASS)
+    passes = channels // K_PASS
+    tiles_per_load = max(BANK_TILES, LOAD_VALUES // channels)
+    load_passes = min(passes, LOAD_VALUES // (BANK_TILES * K_PASS))
     banks = 0
     copied = None
-    for first_tile in range(0, O_TILES, tiles_per_load):
-        tiles = min(tiles_per_load, O_TILES - first_tile)
-        for load_first in range(0, channels // K_PASS, load_passes):
+    for load_tile in range(0, O_TILES, tiles_per_load):
+        tiles = min(tiles_per_load, O_TILES - load_tile)
+        for load_pass in range(0, passes, load_passes):
             raw = pools["w_raw"].tile([P, tiles, load_passes * K_PASS], BF16, tag="w_raw")
             nc.sync.dma_start(
                 out=raw[:],
                 in_=weights[
-                    first_tile * P : (first_tile + tiles) * P, load_first * K_PASS : (load_first + load_passes) * K_PASS
+                    load_tile * P : (load_tile + tiles) * P, load_pass * K_PASS : (load_pass + load_passes) * K_PASS
                 ].rearrange("(t p) c -> p t c", p=P),
             )
-            for t in range(tiles):
-                words = raw[:, t, :].bitcast(F32)
-                for first in range(0, load_passes, BANK_PASSES):
-                    n = min(BANK_PASSES, load_passes - first)
-                    bank = pools["psum"].tile([P, BANK_PASSES, HALVES, P], F32, tag="bank", name="bank")
-                    for i in range(n):
+            for t in range(0, tiles, BANK_TILES):
+                n = min(BANK_TILES, tiles - t)
+                for i in range(load_passes):
+                    bank = pools["psum"].tile([P, BANK_TILES, HALVES, P], F32, tag="bank", name="bank")
+                    for k in range(n):
+                        words = raw[:, t + k, i * K_PASS : (i + 1) * K_PASS].bitcast(F32)
                         for u in range(HALVES):
-                            lo = (first + i) * HALVES * P
-                            nc.tensor.transpose(
-                                out=bank[:, i, u, :], in_=words[:, lo + u : lo + HALVES * P : HALVES], identity=ident[:]
-                            )
-                    grouped = pools["w_grouped"].tile([P, BANK_PASSES, P, PACK], BF16, tag="w_grouped", align_bytes=64)
+                            nc.tensor.transpose(out=bank[:, k, u, :], in_=words[:, u::HALVES], identity=ident[:])
+                    grouped = pools["w_grouped"].tile([P, BANK_TILES, P, PACK], BF16, tag="w_grouped", align_bytes=64)
                     dst = grouped[:, 0:n].bitcast(F32)
-                    src = bank[:, 0:n].rearrange("p g u o -> p g o u")
-                    if banks % 4 == 3:
+                    src = bank[:, 0:n].rearrange("p k u o -> p k o u")
+                    if banks % VECTOR_EVERY == VECTOR_EVERY - 1:
                         nc.vector.tensor_copy(out=dst, in_=src)
                     else:
                         nc.scalar.copy(out=dst, in_=src)
                     banks += 1
                     if copied is not None:
                         quantise_bank(nc, copied, codes, scales)
-                    o_tile = first_tile + t
-                    copied = dict(
-                        grouped=grouped, first=load_first + first, n=n, cols=slice(o_tile * P, (o_tile + 1) * P)
-                    )
+                    first_col = (load_tile + t) * P
+                    copied = dict(grouped=grouped[:, 0:n], g=load_pass + i, cols=slice(first_col, first_col + n * P))
     quantise_bank(nc, copied, codes, scales)
 
 
@@ -283,7 +278,7 @@ def tile_detect_k_kernel(tc, x0, x1, W0, b0, W1, b1, out):
 
         pools = dict(
             psum=psum,
-            w_raw=stack.enter_context(tc.tile_pool(name="w_raw", bufs=6)),
+            w_raw=stack.enter_context(tc.tile_pool(name="w_raw", bufs=3)),
             w_grouped=stack.enter_context(tc.tile_pool(name="w_grouped", bufs=4)),
             x_raw=stack.enter_context(tc.tile_pool(name="x_raw", bufs=8)),
             x_grouped=stack.enter_context(tc.tile_pool(name="x_grouped", bufs=3)),

import math
from contextlib import ExitStack

import concourse.mybir as mybir
from concourse.masks import make_identity

F32 = mybir.dt.float32
BF16 = mybir.dt.bfloat16
I32 = mybir.dt.int32
U32 = mybir.dt.uint32
U8 = mybir.dt.uint8
FP8X4 = mybir.dt.float8_e4m3fn_x4
ALU = mybir.AluOpType
ACT = mybir.ActivationFunctionType

P = 128
PACK = 4
K_PASS = P * PACK
PAIR = 2
HALVES = PACK // PAIR
BATCH = 8
FIELDS = 64
ANGLES = 6
SHAPES = 3
ANCHORS = SHAPES * ANGLES
OUT_CH = ANCHORS * FIELDS
O_TILES = OUT_CH // P
BANK = 512
PSUM_BANKS = 8
CHUNKS = ((0, 512), (512, 512), (1024, 128))
BANK_TILES = BANK // (HALVES * P)
LOAD_VALUES = 8192
VECTOR_EVERY = 6
SLAB = 4
LOAD_AHEAD = 6
REGROUP_AHEAD = 3
QUANTISE_AHEAD = 2
ANGLE_RAD = tuple(math.pi / 180.0 * a for a in (-60.0, -30.0, 0.0, 30.0, 60.0, 90.0))

LEVELS = (
    dict(grid=8, grid_bits=3, stride=8.0, sxy=1.2, shapes=((10, 13), (16, 30), (33, 23)), first_row=0),
    dict(grid=4, grid_bits=2, stride=16.0, sxy=1.1, shapes=((30, 61), (62, 45), (59, 119)), first_row=ANCHORS * 64),
)

FLOPS = 2 * OUT_CH * (8192 * BATCH * 64 + 512 * BATCH * 16)


def anchor_constants(nc, consts, level, cell_index):
    tagged = "L%d" % level["grid"]
    sizes = consts.tile([P, ANCHORS, 2], F32, name="sizes" + tagged)
    for i, (w, h) in enumerate(level["shapes"]):
        nc.vector.memset(sizes[:, i * ANGLES : (i + 1) * ANGLES, 0:1], float(w))
        nc.vector.memset(sizes[:, i * ANGLES : (i + 1) * ANGLES, 1:2], float(h))
    mask = level["grid"] - 1
    cell = consts.tile([P, 2], I32, name="cell" + tagged)
    nc.vector.tensor_single_scalar(out=cell[:, 0:1], in_=cell_index[:], scalar=mask, op=ALU.bitwise_and)
    nc.vector.tensor_scalar(
        out=cell[:, 1:2],
        in0=cell_index[:],
        scalar1=level["grid_bits"],
        scalar2=mask,
        op0=ALU.logical_shift_right,
        op1=ALU.bitwise_and,
    )
    centre = consts.tile([P, 2], F32, name="centre" + tagged)
    nc.vector.tensor_copy(out=centre[:], in_=cell[:])
    nc.vector.tensor_scalar(
        out=centre[:],
        in0=centre[:],
        scalar1=level["stride"],
        scalar2=0.5 * level["stride"],
        op0=ALU.mult,
        op1=ALU.add,
    )
    return sizes, centre


def load_bias_row(nc, consts, level, bias):
    bias_row = consts.tile([P, OUT_CH], BF16, name="bias_rowL%d" % level["grid"])
    nc.vector.memset(bias_row[:].bitcast(I32), 0)
    nc.sync.dma_start(out=bias_row[0:1, :], in_=bias.rearrange("(r o) -> r o", r=1))
    return bias_row


def spread_bias(nc, consts, psum, level, bias_row, ones):
    shift = consts.tile([P, OUT_CH], F32, name="shiftL%d" % level["grid"])
    for start, width in CHUNKS:
        spread = psum.tile([P, BANK], F32, tag="bank", name="spread")
        nc.tensor.matmul(
            out=spread[:, :width], lhsT=ones[:], rhs=bias_row[:, start : start + width], start=True, stop=True
        )
        nc.vector.tensor_copy(out=shift[:, start : start + width], in_=spread[:, :width])
    by_anchor = shift[:].rearrange("p (i j f) -> p i j f", i=SHAPES, j=ANGLES)
    for j, angle in enumerate(ANGLE_RAD):
        nc.vector.tensor_scalar_add(out=by_anchor[:, :, j, 4], in0=by_anchor[:, :, j, 4], scalar1=angle)
    return shift


def quantise_bank(nc, copied, codes, scales):
    nc.vector.quantize_mx(
        out=codes[:, copied["g"], copied["cols"]].bitcast(FP8X4),
        scales=scales[:, copied["g"], copied["cols"]],
        in_=copied["grouped"].rearrange("p k o t -> p (k o t)"),
    )


def quantise_weights(nc, pools, ident, weights, codes, scales):
    channels = weights.shape[1]
    passes = channels // K_PASS
    tiles_per_load = max(BANK_TILES, LOAD_VALUES // channels)
    load_passes = min(passes, LOAD_VALUES // (BANK_TILES * K_PASS))
    banks = 0
    copied = None
    for load_tile in range(0, O_TILES, tiles_per_load):
        tiles = min(tiles_per_load, O_TILES - load_tile)
        for load_pass in range(0, passes, load_passes):
            raw = pools["w_raw"].tile([P, tiles, load_passes * K_PASS], BF16, tag="w_raw")
            nc.sync.dma_start(
                out=raw[:],
                in_=weights[
                    load_tile * P : (load_tile + tiles) * P, load_pass * K_PASS : (load_pass + load_passes) * K_PASS
                ].rearrange("(t p) c -> p t c", p=P),
            )
            for t in range(0, tiles, BANK_TILES):
                n = min(BANK_TILES, tiles - t)
                for i in range(load_passes):
                    bank = pools["psum"].tile([P, BANK_TILES, HALVES, P], F32, tag="bank", name="bank")
                    for k in range(n):
                        words = raw[:, t + k, i * K_PASS : (i + 1) * K_PASS].bitcast(F32)
                        for u in range(HALVES):
                            nc.tensor.transpose(out=bank[:, k, u, :], in_=words[:, u::HALVES], identity=ident[:])
                    grouped = pools["w_grouped"].tile([P, BANK_TILES, P, PACK], BF16, tag="w_grouped", align_bytes=64)
                    dst = grouped[:, 0:n].bitcast(F32)
                    src = bank[:, 0:n].rearrange("p k u o -> p k o u")
                    if banks % VECTOR_EVERY == VECTOR_EVERY - 1:
                        nc.vector.tensor_copy(out=dst, in_=src)
                    else:
                        nc.scalar.copy(out=dst, in_=src)
                    banks += 1
                    if copied is not None:
                        quantise_bank(nc, copied, codes, scales)
                    first_col = (load_tile + t) * P
                    copied = dict(grouped=grouped[:, 0:n], g=load_pass + i, cols=slice(first_col, first_col + n * P))
    quantise_bank(nc, copied, codes, scales)


def load_features(nc, pools, slab):
    job = slab["job"]
    feat = job["feat"]
    cells = job["cells"]
    channels = slice(slab["first"] * K_PASS, (slab["first"] + slab["n"]) * K_PASS)
    for b in job["batches"]:
        raw = pools["x_raw"].tile([P, slab["n"], PACK, cells], BF16, tag="x_raw%d" % cells, name="x_raw")
        nc.sync.dma_start(
            out=raw[:].rearrange("p g t w -> p g (t w)"),
            in_=feat[b, channels].rearrange("(g p t) h w -> p g (t h w)", p=P, t=PACK),
        )
        slab["raw"].append(raw)


def regroup_features(nc, pools, slab):
    cells = slab["job"]["cells"]
    grouped = pools["x_grouped"].tile([P, slab["n"], P, PACK], BF16, tag="x_grouped", align_bytes=64)
    for i, raw in enumerate(slab["raw"]):
        dst = grouped[:, :, i * cells : (i + 1) * cells, :]
        src = raw[:].rearrange("p g t w -> p g w t")
        if i % 2 == 0:
            nc.vector.tensor_copy(out=dst, in_=src)
        else:
            nc.scalar.copy(out=dst, in_=src)
    slab["grouped"] = grouped


def quantise_features(nc, pools, slab):
    job = slab["job"]
    if slab["first"] == 0:
        job["codes"] = pools["x_codes"].tile([P, job["passes"], P], U32, tag="x_codes", name="x_codes", align_bytes=64)
        job["scales"] = pools["x_codes"].tile([P, job["passes"], P], U8, tag="x_scales", name="x_scales", align_bytes=64)
    passes = slice(slab["first"], slab["first"] + slab["n"])
    nc.vector.quantize_mx(
        out=job["codes"][:, passes, :].rearrange("p g c -> p (g c)").bitcast(FP8X4),
        scales=job["scales"][:, passes, :].rearrange("p g c -> p (g c)"),
        in_=slab["grouped"][:].rearrange("p g c t -> p (g c t)"),
    )


def multiply(nc, pools, slab):
    job = slab["job"]
    if slab["first"] == 0:
        job["accs"] = [pools["psum"].tile([P, BANK], F32, tag="bank", name="acc%d" % c) for c in range(len(CHUNKS))]
    for (start, width), acc in zip(CHUNKS, job["accs"]):
        for g in range(slab["first"], slab["first"] + slab["n"]):
            nc.tensor.matmul_mx(
                out=acc[:, :width],
                lhsT=job["codes"][:, g, :].bitcast(FP8X4),
                lhsT_scale=job["scales"][:, g, :],
                rhs=job["w_codes"][:, g, start : start + width].bitcast(FP8X4),
                rhs_scale=job["w_scales"][:, g, start : start + width],
                start=(g == 0),
                stop=(g == job["passes"] - 1),
            )


def decode_first(nc, pools, job):
    work = pools["work"]
    for (start, width), acc in zip(CHUNKS, job["accs"]):
        anchors = width // FIELDS
        dec = work.tile([P, BANK // FIELDS, FIELDS], F32, tag="dec", name="dec", bufs=2 * len(CHUNKS))
        nc.vector.tensor_tensor(
            out=dec[:, 0:anchors].rearrange("p a f -> p (a f)"),
            in0=acc[:, :width],
            in1=job["constants"]["shift"][:, start : start + width],
            op=ALU.add,
        )
        th = work.tile([P, BANK // FIELDS, FIELDS], F32, tag="th", name="th", bufs=len(CHUNKS))
        nc.scalar.activation(out=th[:, 0:anchors], in_=dec[:, 0:anchors], func=ACT.Tanh, scale=0.5)
        grown = work.tile([P, BANK // FIELDS, 2], F32, tag="grown", name="grown", bufs=len(CHUNKS))
        nc.scalar.activation(out=grown[:, 0:anchors], in_=dec[:, 0:anchors, 2:4], func=ACT.Exp)
        job["decoding"].append((dec, th, grown))


def decode_second(nc, job, out):
    level = job["level"]
    cells = job["cells"]
    for (start, width), (dec, th, grown) in zip(CHUNKS, job["decoding"]):
        first_anchor = start // FIELDS
        anchors = width // FIELDS
        nc.vector.tensor_scalar(
            out=dec[:, 0:anchors, 5:FIELDS],
            in0=th[:, 0:anchors, 5:FIELDS],
            scalar1=0.5,
            scalar2=0.5,
            op0=ALU.mult,
            op1=ALU.add,
        )
        nc.vector.scalar_tensor_tensor(
            out=dec[:, 0:anchors, 0:2],
            in0=th[:, 0:anchors, 0:2],
            scalar=0.5 * level["sxy"] * level["stride"],
            in1=job["constants"]["centre"][:].unsqueeze(1).to_broadcast([P, anchors, 2]),
            op0=ALU.mult,
            op1=ALU.add,
        )
        nc.vector.tensor_tensor(
            out=dec[:, 0:anchors, 2:4],
            in0=grown[:, 0:anchors],
            in1=job["constants"]["sizes"][:, first_anchor : first_anchor + anchors, :],
            op=ALU.mult,
        )
        row = level["first_row"] + first_anchor * cells
        for i, b in enumerate(job["batches"]):
            nc.sync.dma_start(
                out=out[b, row : row + anchors * cells, :].rearrange("(a w) f -> w a f", a=anchors),
                in_=dec[i * cells : (i + 1) * cells, 0:anchors, :],
            )


def tile_detect_k_kernel(tc, x0, x1, W0, b0, W1, b1, out):
    nc = tc.nc
    feats = (x0, x1)
    weights = (W0, W1)
    biases = (b0, b1)
    with ExitStack() as stack:
        stack.enter_context(tc.manual_schedule())
        consts = stack.enter_context(tc.tile_pool(name="consts", bufs=1))
        psum = stack.enter_context(tc.psum_pool(name="psum", bufs=PSUM_BANKS))

        bias_rows = [load_bias_row(nc, consts, LEVELS[lv], biases[lv]) for lv in (0, 1)]
        ident = consts.tile([P, P], F32, name="ident")
        make_identity(nc, ident[:])
        ones = consts.tile([P, P], BF16, name="ones")
        nc.vector.memset(ones[:], 1.0)
        cell_index = consts.tile([P, 1], I32, name="cell_index")
        nc.gpsimd.iota(cell_index[:], pattern=[[0, 1]], base=0, channel_multiplier=1)
        anchor_tiles = [anchor_constants(nc, consts, LEVELS[lv], cell_index) for lv in (0, 1)]
        shifts = [spread_bias(nc, consts, psum, LEVELS[lv], bias_rows[lv], ones) for lv in (0, 1)]
        constants = [dict(shift=shifts[lv], sizes=anchor_tiles[lv][0], centre=anchor_tiles[lv][1]) for lv in (0, 1)]

        pools = dict(
            psum=psum,
            w_raw=stack.enter_context(tc.tile_pool(name="w_raw", bufs=3)),
            w_grouped=stack.enter_context(tc.tile_pool(name="w_grouped", bufs=4)),
            x_raw=stack.enter_context(tc.tile_pool(name="x_raw", bufs=8)),
            x_grouped=stack.enter_context(tc.tile_pool(name="x_grouped", bufs=3)),
            x_codes=stack.enter_context(tc.tile_pool(name="x_codes", bufs=2)),
            work=stack.enter_context(tc.tile_pool(name="work", bufs=3)),
        )

        w_codes = [None, None]
        w_scales = [None, None]
        for lv in (1, 0):
            passes = weights[lv].shape[1] // K_PASS
            w_codes[lv] = consts.tile([P, passes, OUT_CH], U32, name="w_codes%d" % lv, align_bytes=64)
            w_scales[lv] = consts.tile([P, passes, OUT_CH], U8, name="w_scales%d" % lv, align_bytes=64)
            quantise_weights(nc, pools, ident, weights[lv], w_codes[lv], w_scales[lv])

        slabs = []
        for lv in (1, 0):
            cells = LEVELS[lv]["grid"] * LEVELS[lv]["grid"]
            passes = feats[lv].shape[1] // K_PASS
            for b in range(0, BATCH, P // cells):
                job = dict(
                    level=LEVELS[lv],
                    constants=constants[lv],
                    feat=feats[lv],
                    cells=cells,
                    passes=passes,
                    batches=range(b, b + P // cells),
                    w_codes=w_codes[lv],
                    w_scales=w_scales[lv],
                    decoding=[],
                )
                for first in range(0, passes, SLAB):
                    n = min(SLAB, passes - first)
                    slabs.append(dict(job=job, first=first, n=n, last=(first + n == passes), raw=[]))

        def slab_at(k):
            return slabs[k] if 0 <= k < len(slabs) else None

        for step in range(-LOAD_AHEAD, len(slabs) + 2):
            if slab_at(step + LOAD_AHEAD) is not None:
                load_features(nc, pools, slab_at(step + LOAD_AHEAD))
            if slab_at(step + QUANTISE_AHEAD) is not None:
                quantise_features(nc, pools, slab_at(step + QUANTISE_AHEAD))
            if slab_at(step + REGROUP_AHEAD) is not None:
                regroup_features(nc, pools, slab_at(step + REGROUP_AHEAD))
            if slab_at(step - 2) is not None and slab_at(step - 2)["last"]:
                decode_second(nc, slab_at(step - 2)["job"], out)
            if slab_at(step) is not None:
                multiply(nc, pools, slab_at(step))
            if slab_at(step - 1) is not None and slab_at(step - 1)["last"]:
                decode_first(nc, pools, slab_at(step - 1)["job"])
